import numpy as np
import ml_dtypes


def mxq(x, axis, fmt="e4m3"):
    dtype, down = {"e4m3": (ml_dtypes.float8_e4m3fn, 7), "e5m2": (ml_dtypes.float8_e5m2, 14)}[fmt]
    v = np.moveaxis(np.asarray(x, np.float32).astype(ml_dtypes.bfloat16).astype(np.float64), axis, -1)
    blocks = v.reshape(v.shape[:-1] + (-1, 32))
    amax = np.abs(blocks).max(-1, keepdims=True)
    byte = np.maximum(np.where(amax > 0, np.frexp(amax)[1] - 1 + 127, 0) - down, 1)
    scale = np.exp2(byte - 127.0)
    codes = (blocks / scale).astype(np.float32).astype(dtype).astype(np.float64)
    return np.moveaxis((codes * scale).reshape(v.shape), -1, axis)


WIDE = False


def mx_kscale(k):
    if not WIDE:
        return np.ones(k)
    levels = np.array([10, -10, 5, -5, 0])
    a = np.random.permutation(np.resize(levels, k // 512 * 4)).reshape(k // 512, 4)
    idx = np.arange(k)
    return np.exp2(a[idx // 512, idx % 128 // 32])


BF16 = ml_dtypes.bfloat16


def bf(x):
    return np.asarray(x, np.float32).astype(BF16)


def f64(x):
    return np.asarray(x).astype(np.float64)


E2M1 = np.array([0.0, 0.5, 1.0, 1.5, 2.0, 3.0, 4.0, 6.0, -0.0, -0.5, -1.0, -1.5, -2.0, -3.0, -4.0, -6.0])


def pack_weight(w, fmt):
    k, n = w.shape
    w = f64(bf(w)).reshape(k // 32, 32, n)
    amax = np.abs(w).max(1)
    if fmt == "e4m3":
        byte = np.frexp(amax)[1] - 1 + 127 - 7
    else:
        mant, ex = np.frexp(amax / 6.0)
        byte = np.where(mant > 0.5, ex, ex - 1) + 127
    byte = np.clip(np.where(amax > 0, byte, 1), 1, 254)
    scaled = (w * np.exp2(127.0 - byte)[:, None, :]).reshape(k, n).astype(np.float32)
    by_word = np.ascontiguousarray(scaled.reshape(k // 512, 128, 4, n).transpose(0, 1, 3, 2))
    if fmt == "e4m3":
        words = by_word.astype(ml_dtypes.float8_e4m3fn).view(np.uint8)
    else:
        c = by_word.astype(ml_dtypes.float4_e2m1fn).view(np.uint8) & 0xF
        words = c[..., 0::2] | (c[..., 1::2] << 4)
    return np.ascontiguousarray(words), np.ascontiguousarray(byte.astype(np.uint8).reshape(k // 512, 16, n))


def unpack_weight(words, scales, fmt):
    g, p, n, _ = words.shape
    if fmt == "e4m3":
        vals = np.ascontiguousarray(words).view(ml_dtypes.float8_e4m3fn).astype(np.float64)
    else:
        nib = np.empty((g, p, n, 4), np.uint8)
        nib[..., 0::2] = words & 0xF
        nib[..., 1::2] = words >> 4
        vals = E2M1[nib]
    vals = vals * np.repeat(np.exp2(scales.astype(np.float64) - 127.0), 8, axis=1)[..., None]
    return vals.transpose(0, 1, 3, 2).reshape(g * 512, n)


B, S, I0, I1, I2, O0, O1, O2 = 1, 128, 1024, 2048, 4096, 2048, 2048, 4608
FMT = "e4m3"


def init_w(out_d, in_d, s):
    w = np.random.uniform(-1.0, 1.0, (out_d, in_d)) / np.sqrt(in_d) / s[None, :in_d]
    return pack_weight(np.ascontiguousarray(w.T), FMT)


def setup_inputs():
    s = mx_kscale(I2)
    x = bf(np.random.standard_normal((B, S, I2)) * s)
    w0_words, w0_scales = init_w(O0, I0, s)
    w1_words, w1_scales = init_w(O1, I1, s)
    w2_words, w2_scales = init_w(O2, I2, s)
    return {"x": x, "W0_words": w0_words, "W0_scales": w0_scales, "W1_words": w1_words, "W1_scales": w1_scales, "W2_words": w2_words, "W2_scales": w2_scales}


def reference(x, W0_words, W0_scales, W1_words, W1_scales, W2_words, W2_scales):
    xq = mxq(f64(x), 2, "e4m3")
    y0 = xq[..., :I0] @ unpack_weight(W0_words, W0_scales, FMT)
    y1 = xq[..., :I1] @ unpack_weight(W1_words, W1_scales, FMT)
    y2 = xq[..., :I2] @ unpack_weight(W2_words, W2_scales, FMT)
    return np.concatenate([y0, y1, y2], axis=-1)

@@ -1,0 +1,138 @@
+from contextlib import ExitStack
+
+import concourse.bass as bass
+import concourse.mybir as mybir
+import concourse.tile as tile
+from concourse.masks import make_identity
+
+F32 = mybir.dt.float32
+BF16 = mybir.dt.bfloat16
+I32 = mybir.dt.int32
+U8 = mybir.dt.uint8
+U32 = mybir.dt.uint32
+FP8X4 = mybir.dt.float8_e4m3fn_x4
+
+P = 128
+FLOPS = 2 * 128 * (1024 * 2048 + 2048 * 2048 + 4096 * 4608)
+
+PIN = True
+SCALES_ON_GPSIMD = False
+W_BUFS = 16
+STAGE_BUFS = 3
+BANK = 512
+
+
+def blocks_of(width):
+    res = []
+    c = 0
+    while c < width:
+        n = min(BANK, width - c)
+        res.append((c, n))
+        c += n
+    return res
+
+
+def tile_naivematryoshkalinear_w_kernel(tc, x, W0_words, W0_scales, W1_words, W1_scales, W2_words, W2_scales, out):
+    nc = tc.nc
+    xf = x.flatten_outer_dims()
+    outf = out.flatten_outer_dims()
+    with ExitStack() as ctx:
+        const = ctx.enter_context(tc.tile_pool(name="const", bufs=1))
+        wpool = ctx.enter_context(tc.tile_pool(name="w", bufs=W_BUFS))
+        spool = ctx.enter_context(tc.tile_pool(name="stage", bufs=STAGE_BUFS))
+        psum = ctx.enter_context(tc.psum_pool(name="psum", bufs=8))
+        if PIN:
+            ctx.enter_context(tc.manual_schedule())
+
+        x_sb = const.tile([P, 4096], BF16, name="x_sb", align_bytes=64)
+        nc.sync.dma_start(out=x_sb[:], in_=xf)
+
+        pl2a = const.tile([P, 4608], U8, name="pl2a", align_bytes=64)
+        pl2b = const.tile([P, 4608], U8, name="pl2b", align_bytes=64)
+        pl1 = const.tile([P, 2048], U8, name="pl1", align_bytes=64)
+        pl0 = const.tile([P, 2048], U8, name="pl0", align_bytes=64)
+        for pl in (pl2a, pl2b, pl1, pl0):
+            nc.vector.memset(pl[:].bitcast(I32), 0)
+
+        ident = const.tile([P, P], F32, name="ident")
+        make_identity(nc, ident[:])
+
+        def load_planes(pl, scales, g0, count):
+            for q in range(4):
+                dst = pl[32 * q : 32 * q + 4 * count, :]
+                src = scales[g0 : g0 + count, 4 * q : 4 * q + 4, :]
+                if SCALES_ON_GPSIMD:
+                    nc.gpsimd.dma_start(out=dst.bitcast(F32), in_=src.bitcast(F32))
+                else:
+                    nc.sync.dma_start(out=dst.bitcast(I32), in_=src.bitcast(I32))
+
+        load_planes(pl2a, W2_scales, 0, 4)
+        load_planes(pl2b, W2_scales, 4, 4)
+        load_planes(pl1, W1_scales, 0, 4)
+        load_planes(pl0, W0_scales, 0, 2)
+
+        grouped = const.tile([P, 8, P, 4], BF16, name="grouped", align_bytes=64)
+        x_codes = const.tile([P, 8 * P], U32, name="x_codes", align_bytes=64)
+        x_plane = const.tile([P, 8 * P], U8, name="x_plane", align_bytes=64)
+        xw = x_sb[:].bitcast(F32)
+        for b in range(4):
+            xt = psum.tile([P, 2, 2, P], F32, name="xt", tag="bank")
+            for gg in range(2):
+                g = 2 * b + gg
+                for u in range(2):
+                    nc.tensor.transpose(xt[:, gg, u, :], xw[:, 256 * g + u : 256 * (g + 1) : 2], ident[:])
+            dst = grouped[:, 2 * b : 2 * b + 2].bitcast(F32)
+            src = xt[:].rearrange("p g u m -> p g m u")
+            if b % 2 == 0:
+                nc.vector.tensor_copy(out=dst, in_=src)
+            else:
+                nc.scalar.copy(out=dst, in_=src)
+        for b in range(4):
+            nc.vector.quantize_mx(
+                out=x_codes[:, 256 * b : 256 * (b + 1)].bitcast(FP8X4),
+                scales=x_plane[:, 256 * b : 256 * (b + 1)],
+                in_=grouped[:, 2 * b : 2 * b + 2].rearrange("p g m t -> p (g m t)"),
+            )
+
+        state = {"copies": 0}
+
+        def run_round(words, n_groups, plane_of, c0, width, out_c0, last_pieces):
+            blks = blocks_of(width)
+            accs = [psum.tile([P, BANK], F32, name="acc", tag="bank") for blk in blks]
+            for g in range(n_groups):
+                last = g == n_groups - 1
+                pieces = last_pieces if last else [(0, width)]
+                pl, k = plane_of(g)
+                for pc0, pw in pieces:
+                    wt = wpool.tile([P, 4 * pw], U8, name="wt", tag="w", align_bytes=64)
+                    src = words[g].rearrange("p n t -> p (n t)")[:, 4 * (c0 + pc0) : 4 * (c0 + pc0 + pw)]
+                    nc.sync.dma_start(out=wt[:].bitcast(I32), in_=src.bitcast(I32))
+                    mine = [(i, bc, n) for i, (bc, n) in enumerate(blks) if pc0 <= bc < pc0 + pw]
+                    for i, bc, n in mine:
+                        nc.tensor.matmul_mx(
+                            out=accs[i][:, :n],
+                            lhsT=x_codes[:, P * g : P * (g + 1)].bitcast(FP8X4),
+                            lhsT_scale=x_plane[:, P * g : P * (g + 1)],
+                            rhs=wt[:, 4 * (bc - pc0) : 4 * (bc - pc0 + n)].bitcast(FP8X4),
+                            rhs_scale=pl[k:P, c0 + bc : c0 + bc + n],
+                            start=(g == 0),
+                            stop=last,
+                        )
+                    if last:
+                        st = spool.tile([P, pw], F32, name="st", tag="stage")
+                        for i, bc, n in mine:
+                            dst = st[:, bc - pc0 : bc - pc0 + n]
+                            if state["copies"] % 2 == 0:
+                                nc.vector.tensor_copy(out=dst, in_=accs[i][:, :n])
+                            else:
+                                nc.scalar.copy(out=dst, in_=accs[i][:, :n])
+                            state["copies"] += 1
+                        nc.scalar.dma_start(out=outf[:, out_c0 + pc0 : out_c0 + pc0 + pw], in_=st[:])
+
+        def plane2(g):
+            return (pl2a if g < 4 else pl2b), 4 * (g % 4)
+
+        run_round(W2_words, 8, plane2, 0, 2304, 4096, [(0, 2304)])
+        run_round(W2_words, 8, plane2, 2304, 2304, 4096 + 2304, [(0, 2304)])
+        run_round(W1_words, 4, lambda g: (pl1, 4 * g), 0, 2048, 2048, [(0, 2048)])
+        run_round(W0_words, 2, lambda g: (pl0, 4 * g), 0, 2048, 0, [(0, 1024), (1024, 512), (1536, 512)])

@@ -16,7 +16,7 @@ P = 128
 FLOPS = 2 * 128 * (1024 * 2048 + 2048 * 2048 + 4096 * 4608)
 
 PIN = True
-SCALES_ON_GPSIMD = False
+SCALES_ON_GPSIMD = True
 W_BUFS = 16
 STAGE_BUFS = 3
 BANK = 512

@@ -16,9 +16,9 @@ P = 128
 FLOPS = 2 * 128 * (1024 * 2048 + 2048 * 2048 + 4096 * 4608)
 
 PIN = True
-SCALES_ON_GPSIMD = True
+SCALES_ON_GPSIMD = False
 W_BUFS = 16
-STAGE_BUFS = 3
+STAGE_BUFS = 1
 BANK = 512
 
 
@@ -94,9 +94,10 @@ def tile_naivematryoshkalinear_w_kernel(tc, x, W0_words, W0_scales, W1_words, W1
                 in_=grouped[:, 2 * b : 2 * b + 2].rearrange("p g m t -> p (g m t)"),
             )
 
-        state = {"copies": 0}
+        state = {"copies": 0, "stages": 0}
+        late_stores = []
 
-        def run_round(words, n_groups, plane_of, c0, width, out_c0, last_pieces):
+        def run_round(words, n_groups, plane_of, c0, width, out_c0, last_pieces, defer):
             blks = blocks_of(width)
             accs = [psum.tile([P, BANK], F32, name="acc", tag="bank") for blk in blks]
             for g in range(n_groups):
@@ -119,7 +120,8 @@ def tile_naivematryoshkalinear_w_kernel(tc, x, W0_words, W0_scales, W1_words, W1
                             stop=last,
                         )
                     if last:
-                        st = spool.tile([P, pw], F32, name="st", tag="stage")
+                        st = spool.tile([P, pw], F32, name="st", tag="st%d" % state["stages"])
+                        state["stages"] += 1
                         for i, bc, n in mine:
                             dst = st[:, bc - pc0 : bc - pc0 + n]
                             if state["copies"] % 2 == 0:
@@ -127,12 +129,18 @@ def tile_naivematryoshkalinear_w_kernel(tc, x, W0_words, W0_scales, W1_words, W1
                             else:
                                 nc.scalar.copy(out=dst, in_=accs[i][:, :n])
                             state["copies"] += 1
-                        nc.scalar.dma_start(out=outf[:, out_c0 + pc0 : out_c0 + pc0 + pw], in_=st[:])
+                        dst_out = outf[:, out_c0 + pc0 : out_c0 + pc0 + pw]
+                        if defer:
+                            late_stores.append((dst_out, st))
+                        else:
+                            nc.scalar.dma_start(out=dst_out, in_=st[:])
 
         def plane2(g):
             return (pl2a if g < 4 else pl2b), 4 * (g % 4)
 
-        run_round(W2_words, 8, plane2, 0, 2304, 4096, [(0, 2304)])
-        run_round(W2_words, 8, plane2, 2304, 2304, 4096 + 2304, [(0, 2304)])
-        run_round(W1_words, 4, lambda g: (pl1, 4 * g), 0, 2048, 2048, [(0, 2048)])
-        run_round(W0_words, 2, lambda g: (pl0, 4 * g), 0, 2048, 0, [(0, 1024), (1024, 512), (1536, 512)])
+        run_round(W2_words, 8, plane2, 0, 2304, 4096, [(0, 2304)], False)
+        run_round(W2_words, 8, plane2, 2304, 2304, 4096 + 2304, [(0, 2304)], True)
+        run_round(W1_words, 4, lambda g: (pl1, 4 * g), 0, 2048, 2048, [(0, 2048)], True)
+        run_round(W0_words, 2, lambda g: (pl0, 4 * g), 0, 2048, 0, [(0, 1024), (1024, 512), (1536, 512)], True)
+        for dst_out, st in late_stores:
+            nc.sync.dma_start(out=dst_out, in_=st[:])

@@ -57,19 +57,16 @@ def tile_naivematryoshkalinear_w_kernel(tc, x, W0_words, W0_scales, W1_words, W1
         ident = const.tile([P, P], F32, name="ident")
         make_identity(nc, ident[:])
 
-        def load_planes(pl, scales, g0, count):
-            for q in range(4):
-                dst = pl[32 * q : 32 * q + 4 * count, :]
-                src = scales[g0 : g0 + count, 4 * q : 4 * q + 4, :]
-                if SCALES_ON_GPSIMD:
-                    nc.gpsimd.dma_start(out=dst.bitcast(F32), in_=src.bitcast(F32))
-                else:
-                    nc.sync.dma_start(out=dst.bitcast(I32), in_=src.bitcast(I32))
+        def load_plane_quadrant(pl, scales, g0, count, q):
+            dst = pl[32 * q : 32 * q + 4 * count, :]
+            src = scales[g0 : g0 + count, 4 * q : 4 * q + 4, :]
+            nc.sync.dma_start(out=dst.bitcast(I32), in_=src.bitcast(I32))
 
-        load_planes(pl2a, W2_scales, 0, 4)
-        load_planes(pl2b, W2_scales, 4, 4)
-        load_planes(pl1, W1_scales, 0, 4)
-        load_planes(pl0, W0_scales, 0, 2)
+        plane_sets = [(pl2a, W2_scales, 0, 4), (pl2b, W2_scales, 4, 4), (pl1, W1_scales, 0, 4), (pl0, W0_scales, 0, 2)]
+        for quadrants in ((2, 3), (0, 1)):
+            for pl, scales, g0, count in plane_sets:
+                for q in quadrants:
+                    load_plane_quadrant(pl, scales, g0, count, q)
 
         grouped = const.tile([P, 8, P, 4], BF16, name="grouped", align_bytes=64)
         x_codes = const.tile([P, 8 * P], U32, name="x_codes", align_bytes=64)

@@ -1,8 +1,6 @@
 from contextlib import ExitStack
 
-import concourse.bass as bass
 import concourse.mybir as mybir
-import concourse.tile as tile
 from concourse.masks import make_identity
 
 F32 = mybir.dt.float32
@@ -13,23 +11,8 @@ U32 = mybir.dt.uint32
 FP8X4 = mybir.dt.float8_e4m3fn_x4
 
 P = 128
-FLOPS = 2 * 128 * (1024 * 2048 + 2048 * 2048 + 4096 * 4608)
-
-PIN = True
-SCALES_ON_GPSIMD = False
-W_BUFS = 16
-STAGE_BUFS = 1
 BANK = 512
-
-
-def blocks_of(width):
-    res = []
-    c = 0
-    while c < width:
-        n = min(BANK, width - c)
-        res.append((c, n))
-        c += n
-    return res
+FLOPS = 2 * 128 * (1024 * 2048 + 2048 * 2048 + 4096 * 4608)
 
 
 def tile_naivematryoshkalinear_w_kernel(tc, x, W0_words, W0_scales, W1_words, W1_scales, W2_words, W2_scales, out):
@@ -38,14 +21,16 @@ def tile_naivematryoshkalinear_w_kernel(tc, x, W0_words, W0_scales, W1_words, W1
     outf = out.flatten_outer_dims()
     with ExitStack() as ctx:
         const = ctx.enter_context(tc.tile_pool(name="const", bufs=1))
-        wpool = ctx.enter_context(tc.tile_pool(name="w", bufs=W_BUFS))
-        spool = ctx.enter_context(tc.tile_pool(name="stage", bufs=STAGE_BUFS))
+        xs = ctx.enter_context(tc.tile_pool(name="xs", bufs=1))
+        w2pool = ctx.enter_context(tc.tile_pool(name="w2", bufs=8))
+        wsmall = ctx.enter_context(tc.tile_pool(name="ws", bufs=1))
         psum = ctx.enter_context(tc.psum_pool(name="psum", bufs=8))
-        if PIN:
-            ctx.enter_context(tc.manual_schedule())
+        ctx.enter_context(tc.manual_schedule())
 
-        x_sb = const.tile([P, 4096], BF16, name="x_sb", align_bytes=64)
-        nc.sync.dma_start(out=x_sb[:], in_=xf)
+        xg = xs.tile([P, 8192], BF16, name="xg", tag="xs", align_bytes=64)
+        x_sb = xg[:, 0:4096]
+        grouped = xg[:, 4096:8192].rearrange("p (g m t) -> p g m t", g=8, m=P, t=4)
+        nc.sync.dma_start(out=x_sb, in_=xf)
 
         pl2a = const.tile([P, 4608], U8, name="pl2a", align_bytes=64)
         pl2b = const.tile([P, 4608], U8, name="pl2b", align_bytes=64)
@@ -68,10 +53,29 @@ def tile_naivematryoshkalinear_w_kernel(tc, x, W0_words, W0_scales, W1_words, W1
                 for q in quadrants:
                     load_plane_quadrant(pl, scales, g0, count, q)
 
-        grouped = const.tile([P, 8, P, 4], BF16, name="grouped", align_bytes=64)
+        w2t = []
+        for g in range(8):
+            wt = w2pool.tile([P, 4 * 4608], U8, name="w2t", tag="w2", align_bytes=64)
+            nc.sync.dma_start(out=wt[:].bitcast(I32), in_=W2_words[g].rearrange("p n t -> p (n t)").bitcast(I32))
+            w2t.append(wt)
+        w1t = []
+        for a in range(2):
+            wt = wsmall.tile([P, 2, 4 * 2048], U8, name="w1t%d" % a, tag="w1t%d" % a, align_bytes=64)
+            nc.sync.dma_start(out=wt[:].bitcast(I32), in_=W1_words[2 * a : 2 * a + 2].rearrange("g p n t -> p g (n t)").bitcast(I32))
+            w1t.append(wt)
+        w0first = wsmall.tile([P, 4 * 2048], U8, name="w0first", tag="w0first", align_bytes=64)
+        nc.sync.dma_start(out=w0first[:].bitcast(I32), in_=W0_words[0].rearrange("p n t -> p (n t)").bitcast(I32))
+        last_pieces = [(0, 1024), (1024, 512), (1536, 512)]
+        w0last = []
+        for i, (c0, width) in enumerate(last_pieces):
+            wt = wsmall.tile([P, 4 * width], U8, name="w0last%d" % i, tag="w0last%d" % i, align_bytes=64)
+            src = W0_words[1].rearrange("p n t -> p (n t)")[:, 4 * c0 : 4 * (c0 + width)]
+            nc.sync.dma_start(out=wt[:].bitcast(I32), in_=src.bitcast(I32))
+            w0last.append(wt)
+
         x_codes = const.tile([P, 8 * P], U32, name="x_codes", align_bytes=64)
         x_plane = const.tile([P, 8 * P], U8, name="x_plane", align_bytes=64)
-        xw = x_sb[:].bitcast(F32)
+        xw = x_sb.bitcast(F32)
         for b in range(4):
             xt = psum.tile([P, 2, 2, P], F32, name="xt", tag="bank")
             for gg in range(2):
@@ -88,56 +92,68 @@ def tile_naivematryoshkalinear_w_kernel(tc, x, W0_words, W0_scales, W1_words, W1
             nc.vector.quantize_mx(
                 out=x_codes[:, 256 * b : 256 * (b + 1)].bitcast(FP8X4),
                 scales=x_plane[:, 256 * b : 256 * (b + 1)],
-                in_=grouped[:, 2 * b : 2 * b + 2].rearrange("p g m t -> p (g m t)"),
+                in_=xg[:, 4096 + 1024 * b : 4096 + 1024 * (b + 1)],
             )
 
-        state = {"copies": 0, "stages": 0}
-        late_stores = []
+        state = {"copies": 0}
 
-        def run_round(words, n_groups, plane_of, c0, width, out_c0, last_pieces, defer):
-            blks = blocks_of(width)
-            accs = [psum.tile([P, BANK], F32, name="acc", tag="bank") for blk in blks]
-            for g in range(n_groups):
-                last = g == n_groups - 1
-                pieces = last_pieces if last else [(0, width)]
-                pl, k = plane_of(g)
-                for pc0, pw in pieces:
-                    wt = wpool.tile([P, 4 * pw], U8, name="wt", tag="w", align_bytes=64)
-                    src = words[g].rearrange("p n t -> p (n t)")[:, 4 * (c0 + pc0) : 4 * (c0 + pc0 + pw)]
-                    nc.sync.dma_start(out=wt[:].bitcast(I32), in_=src.bitcast(I32))
-                    mine = [(i, bc, n) for i, (bc, n) in enumerate(blks) if pc0 <= bc < pc0 + pw]
-                    for i, bc, n in mine:
-                        nc.tensor.matmul_mx(
-                            out=accs[i][:, :n],
-                            lhsT=x_codes[:, P * g : P * (g + 1)].bitcast(FP8X4),
-                            lhsT_scale=x_plane[:, P * g : P * (g + 1)],
-                            rhs=wt[:, 4 * (bc - pc0) : 4 * (bc - pc0 + n)].bitcast(FP8X4),
-                            rhs_scale=pl[k:P, c0 + bc : c0 + bc + n],
-                            start=(g == 0),
-                            stop=last,
-                        )
-                    if last:
-                        st = spool.tile([P, pw], F32, name="st", tag="st%d" % state["stages"])
-                        state["stages"] += 1
-                        for i, bc, n in mine:
-                            dst = st[:, bc - pc0 : bc - pc0 + n]
-                            if state["copies"] % 2 == 0:
-                                nc.vector.tensor_copy(out=dst, in_=accs[i][:, :n])
-                            else:
-                                nc.scalar.copy(out=dst, in_=accs[i][:, :n])
-                            state["copies"] += 1
-                        dst_out = outf[:, out_c0 + pc0 : out_c0 + pc0 + pw]
-                        if defer:
-                            late_stores.append((dst_out, st))
-                        else:
-                            nc.scalar.dma_start(out=dst_out, in_=st[:])
+        def mx_pass(acc, g, codes, plane, first, last):
+            nc.tensor.matmul_mx(
+                out=acc,
+                lhsT=x_codes[:, P * g : P * (g + 1)].bitcast(FP8X4),
+                lhsT_scale=x_plane[:, P * g : P * (g + 1)],
+                rhs=codes.bitcast(FP8X4),
+                rhs_scale=plane,
+                start=first,
+                stop=last,
+            )
 
-        def plane2(g):
-            return (pl2a if g < 4 else pl2b), 4 * (g % 4)
+        def leave_psum(dst, acc):
+            if state["copies"] % 2 == 0:
+                nc.vector.tensor_copy(out=dst, in_=acc)
+            else:
+                nc.scalar.copy(out=dst, in_=acc)
+            state["copies"] += 1
 
-        run_round(W2_words, 8, plane2, 0, 2304, 4096, [(0, 2304)], False)
-        run_round(W2_words, 8, plane2, 2304, 2304, 4096 + 2304, [(0, 2304)], True)
-        run_round(W1_words, 4, lambda g: (pl1, 4 * g), 0, 2048, 2048, [(0, 2048)], True)
-        run_round(W0_words, 2, lambda g: (pl0, 4 * g), 0, 2048, 0, [(0, 1024), (1024, 512), (1536, 512)], True)
-        for dst_out, st in late_stores:
-            nc.sync.dma_start(out=dst_out, in_=st[:])
+        def plane2(g, c0):
+            pl = pl2a if g < 4 else pl2b
+            return pl[4 * (g % 4) : P, c0 : c0 + BANK]
+
+        accs = [psum.tile([P, BANK], F32, name="acc", tag="bank") for blk in range(8)]
+        for g in range(8):
+            for blk in range(8):
+                c0 = BANK * blk
+                mx_pass(accs[blk][:], g, w2t[g][:, 4 * c0 : 4 * (c0 + BANK)], plane2(g, c0), g == 0, g == 7)
+        st_main = xs.tile([P, 4096], F32, name="st_main", tag="xs", align_bytes=64)
+        for blk in range(8):
+            leave_psum(st_main[:, BANK * blk : BANK * (blk + 1)], accs[blk][:])
+
+        acc8 = psum.tile([P, BANK], F32, name="acc", tag="bank")
+        for g in range(8):
+            mx_pass(acc8[:], g, w2t[g][:, 4 * 4096 : 4 * 4608], plane2(g, 4096), g == 0, g == 7)
+        st_late = w2pool.tile([P, 4608], F32, name="st_late", tag="w2", align_bytes=64)
+        leave_psum(st_late[:, 4096:4608], acc8[:])
+
+        accs = [psum.tile([P, BANK], F32, name="acc", tag="bank") for blk in range(4)]
+        for g in range(4):
+            for blk in range(4):
+                c0 = BANK * blk
+                mx_pass(accs[blk][:], g, w1t[g // 2][:, g % 2, 4 * c0 : 4 * (c0 + BANK)], pl1[4 * g : P, c0 : c0 + BANK], g == 0, g == 3)
+        for blk in range(4):
+            leave_psum(st_late[:, 2048 + BANK * blk : 2048 + BANK * (blk + 1)], accs[blk][:])
+
+        accs = [psum.tile([P, BANK], F32, name="acc", tag="bank") for blk in range(4)]
+        for blk in range(4):
+            c0 = BANK * blk
+            mx_pass(accs[blk][:], 0, w0first[:, 4 * c0 : 4 * (c0 + BANK)], pl0[0:P, c0 : c0 + BANK], True, False)
+        for (p0, width), wt in zip(last_pieces, w0last):
+            for c0 in range(p0, p0 + width, BANK):
+                mx_pass(accs[c0 // BANK][:], 1, wt[:, 4 * (c0 - p0) : 4 * (c0 - p0 + BANK)], pl0[4:P, c0 : c0 + BANK], False, True)
+            for c0 in range(p0, p0 + width, BANK):
+                leave_psum(st_late[:, c0 : c0 + BANK], accs[c0 // BANK][:])
+
+        nc.sync.dma_start(out=outf[:, 4096:8192], in_=st_main[:])
+        nc.sync.dma_start(out=outf[:, 8192:8704], in_=st_late[:, 4096:4608])
+        nc.sync.dma_start(out=outf[:, 2048:4096], in_=st_late[:, 2048:4096])
+        for p0, width in last_pieces:
+            nc.sync.dma_start(out=outf[:, p0 : p0 + width], in_=st_late[:, p0 : p0 + width])

@@ -42,16 +42,19 @@ def tile_naivematryoshkalinear_w_kernel(tc, x, W0_words, W0_scales, W1_words, W1
         ident = const.tile([P, P], F32, name="ident")
         make_identity(nc, ident[:])
 
-        def load_plane_quadrant(pl, scales, g0, count, q):
+        def load_plane_quadrant(pl, scales, g0, count, q, software):
             dst = pl[32 * q : 32 * q + 4 * count, :]
             src = scales[g0 : g0 + count, 4 * q : 4 * q + 4, :]
-            nc.sync.dma_start(out=dst.bitcast(I32), in_=src.bitcast(I32))
+            if software:
+                nc.gpsimd.dma_start(out=dst.bitcast(F32), in_=src.bitcast(F32))
+            else:
+                nc.sync.dma_start(out=dst.bitcast(I32), in_=src.bitcast(I32))
 
         plane_sets = [(pl2a, W2_scales, 0, 4), (pl2b, W2_scales, 4, 4), (pl1, W1_scales, 0, 4), (pl0, W0_scales, 0, 2)]
         for quadrants in ((2, 3), (0, 1)):
             for pl, scales, g0, count in plane_sets:
                 for q in quadrants:
-                    load_plane_quadrant(pl, scales, g0, count, q)
+                    load_plane_quadrant(pl, scales, g0, count, q, q < 2 and scales is W2_scales)
 
         w2t = []
         for g in range(8):

@@ -68,13 +68,8 @@ def tile_naivematryoshkalinear_w_kernel(tc, x, W0_words, W0_scales, W1_words, W1
             w1t.append(wt)
         w0first = wsmall.tile([P, 4 * 2048], U8, name="w0first", tag="w0first", align_bytes=64)
         nc.sync.dma_start(out=w0first[:].bitcast(I32), in_=W0_words[0].rearrange("p n t -> p (n t)").bitcast(I32))
-        last_pieces = [(0, 1024), (1024, 512), (1536, 512)]
-        w0last = []
-        for i, (c0, width) in enumerate(last_pieces):
-            wt = wsmall.tile([P, 4 * width], U8, name="w0last%d" % i, tag="w0last%d" % i, align_bytes=64)
-            src = W0_words[1].rearrange("p n t -> p (n t)")[:, 4 * c0 : 4 * (c0 + width)]
-            nc.sync.dma_start(out=wt[:].bitcast(I32), in_=src.bitcast(I32))
-            w0last.append(wt)
+        w0last = wsmall.tile([P, 4 * 2048], U8, name="w0last", tag="w0last", align_bytes=64)
+        nc.sync.dma_start(out=w0last[:].bitcast(I32), in_=W0_words[1].rearrange("p n t -> p (n t)").bitcast(I32))
 
         x_codes = const.tile([P, 8 * P], U32, name="x_codes", align_bytes=64)
         x_plane = const.tile([P, 8 * P], U8, name="x_plane", align_bytes=64)
@@ -127,15 +122,15 @@ def tile_naivematryoshkalinear_w_kernel(tc, x, W0_words, W0_scales, W1_words, W1
             for blk in range(8):
                 c0 = BANK * blk
                 mx_pass(accs[blk][:], g, w2t[g][:, 4 * c0 : 4 * (c0 + BANK)], plane2(g, c0), g == 0, g == 7)
-        st_main = xs.tile([P, 4096], F32, name="st_main", tag="xs", align_bytes=64)
+        st_main = xs.tile([P, 4608], F32, name="st_main", tag="xs", align_bytes=64)
         for blk in range(8):
             leave_psum(st_main[:, BANK * blk : BANK * (blk + 1)], accs[blk][:])
 
         acc8 = psum.tile([P, BANK], F32, name="acc", tag="bank")
         for g in range(8):
             mx_pass(acc8[:], g, w2t[g][:, 4 * 4096 : 4 * 4608], plane2(g, 4096), g == 0, g == 7)
-        st_late = w2pool.tile([P, 4608], F32, name="st_late", tag="w2", align_bytes=64)
-        leave_psum(st_late[:, 4096:4608], acc8[:])
+        leave_psum(st_main[:, 4096:4608], acc8[:])
+        st_late = w2pool.tile([P, 4096], F32, name="st_late", tag="w2", align_bytes=64)
 
         accs = [psum.tile([P, BANK], F32, name="acc", tag="bank") for blk in range(4)]
         for g in range(4):
@@ -149,14 +144,11 @@ def tile_naivematryoshkalinear_w_kernel(tc, x, W0_words, W0_scales, W1_words, W1
         for blk in range(4):
             c0 = BANK * blk
             mx_pass(accs[blk][:], 0, w0first[:, 4 * c0 : 4 * (c0 + BANK)], pl0[0:P, c0 : c0 + BANK], True, False)
-        for (p0, width), wt in zip(last_pieces, w0last):
-            for c0 in range(p0, p0 + width, BANK):
-                mx_pass(accs[c0 // BANK][:], 1, wt[:, 4 * (c0 - p0) : 4 * (c0 - p0 + BANK)], pl0[4:P, c0 : c0 + BANK], False, True)
-            for c0 in range(p0, p0 + width, BANK):
-                leave_psum(st_late[:, c0 : c0 + BANK], accs[c0 // BANK][:])
+        for blk in range(4):
+            c0 = BANK * blk
+            mx_pass(accs[blk][:], 1, w0last[:, 4 * c0 : 4 * (c0 + BANK)], pl0[4:P, c0 : c0 + BANK], False, True)
+            leave_psum(st_late[:, c0 : c0 + BANK], accs[blk][:])
 
-        nc.sync.dma_start(out=outf[:, 4096:8192], in_=st_main[:])
-        nc.sync.dma_start(out=outf[:, 8192:8704], in_=st_late[:, 4096:4608])
+        nc.sync.dma_start(out=outf[:, 4096:8704], in_=st_main[:])
         nc.sync.dma_start(out=outf[:, 2048:4096], in_=st_late[:, 2048:4096])
-        for p0, width in last_pieces:
-            nc.sync.dma_start(out=outf[:, p0 : p0 + width], in_=st_late[:, p0 : p0 + width])
+        nc.sync.dma_start(out=outf[:, 0:2048], in_=st_late[:, 0:2048])

@@ -22,7 +22,7 @@ def tile_naivematryoshkalinear_w_kernel(tc, x, W0_words, W0_scales, W1_words, W1
     with ExitStack() as ctx:
         const = ctx.enter_context(tc.tile_pool(name="const", bufs=1))
         xs = ctx.enter_context(tc.tile_pool(name="xs", bufs=1))
-        w2pool = ctx.enter_context(tc.tile_pool(name="w2", bufs=8))
+        w2pool = ctx.enter_context(tc.tile_pool(name="w2", bufs=4))
         wsmall = ctx.enter_context(tc.tile_pool(name="ws", bufs=1))
         psum = ctx.enter_context(tc.psum_pool(name="psum", bufs=8))
         ctx.enter_context(tc.manual_schedule())
@@ -57,9 +57,9 @@ def tile_naivematryoshkalinear_w_kernel(tc, x, W0_words, W0_scales, W1_words, W1
                     load_plane_quadrant(pl, scales, g0, count, q, q < 2 and scales is W2_scales)
 
         w2t = []
-        for g in range(8):
-            wt = w2pool.tile([P, 4 * 4608], U8, name="w2t", tag="w2", align_bytes=64)
-            nc.sync.dma_start(out=wt[:].bitcast(I32), in_=W2_words[g].rearrange("p n t -> p (n t)").bitcast(I32))
+        for a in range(4):
+            wt = w2pool.tile([P, 2, 4 * 4608], U8, name="w2t", tag="w2", align_bytes=64)
+            nc.sync.dma_start(out=wt[:].bitcast(I32), in_=W2_words[2 * a : 2 * a + 2].rearrange("g p n t -> p g (n t)").bitcast(I32))
             w2t.append(wt)
         w1t = []
         for a in range(2):
@@ -121,14 +121,14 @@ def tile_naivematryoshkalinear_w_kernel(tc, x, W0_words, W0_scales, W1_words, W1
         for g in range(8):
             for blk in range(8):
                 c0 = BANK * blk
-                mx_pass(accs[blk][:], g, w2t[g][:, 4 * c0 : 4 * (c0 + BANK)], plane2(g, c0), g == 0, g == 7)
+                mx_pass(accs[blk][:], g, w2t[g // 2][:, g % 2, 4 * c0 : 4 * (c0 + BANK)], plane2(g, c0), g == 0, g == 7)
         st_main = xs.tile([P, 4608], F32, name="st_main", tag="xs", align_bytes=64)
         for blk in range(8):
             leave_psum(st_main[:, BANK * blk : BANK * (blk + 1)], accs[blk][:])
 
         acc8 = psum.tile([P, BANK], F32, name="acc", tag="bank")
         for g in range(8):
-            mx_pass(acc8[:], g, w2t[g][:, 4 * 4096 : 4 * 4608], plane2(g, 4096), g == 0, g == 7)
+            mx_pass(acc8[:], g, w2t[g // 2][:, g % 2, 4 * 4096 : 4 * 4608], plane2(g, 4096), g == 0, g == 7)
         leave_psum(st_main[:, 4096:4608], acc8[:])
         st_late = w2pool.tile([P, 4096], F32, name="st_late", tag="w2", align_bytes=64)
 

@@ -36,7 +36,7 @@ def tile_naivematryoshkalinear_w_kernel(tc, x, W0_words, W0_scales, W1_words, W1
         pl2b = const.tile([P, 4608], U8, name="pl2b", align_bytes=64)
         pl1 = const.tile([P, 2048], U8, name="pl1", align_bytes=64)
         pl0 = const.tile([P, 2048], U8, name="pl0", align_bytes=64)
-        for pl in (pl2a, pl2b, pl1, pl0):
+        for pl in (pl2a, pl1, pl0, pl2b):
             nc.vector.memset(pl[:].bitcast(I32), 0)
 
         ident = const.tile([P, P], F32, name="ident")
@@ -50,11 +50,18 @@ def tile_naivematryoshkalinear_w_kernel(tc, x, W0_words, W0_scales, W1_words, W1
             else:
                 nc.sync.dma_start(out=dst.bitcast(I32), in_=src.bitcast(I32))
 
-        plane_sets = [(pl2a, W2_scales, 0, 4), (pl2b, W2_scales, 4, 4), (pl1, W1_scales, 0, 4), (pl0, W0_scales, 0, 2)]
-        for quadrants in ((2, 3), (0, 1)):
-            for pl, scales, g0, count in plane_sets:
-                for q in quadrants:
-                    load_plane_quadrant(pl, scales, g0, count, q, q < 2 and scales is W2_scales)
+        first_half = [(pl2a, W2_scales, 0, 4), (pl1, W1_scales, 0, 4), (pl0, W0_scales, 0, 2)]
+        second_half = [(pl2b, W2_scales, 4, 4), (pl1, W1_scales, 0, 4), (pl0, W0_scales, 0, 2)]
+        for pl, scales, g0, count in first_half:
+            for q in (2, 3):
+                load_plane_quadrant(pl, scales, g0, count, q, False)
+        for q in (0, 1):
+            load_plane_quadrant(pl2a, W2_scales, 0, 4, q, True)
+        for pl, scales, g0, count in second_half:
+            for q in (0, 1):
+                load_plane_quadrant(pl, scales, g0, count, q, False)
+        for q in (2, 3):
+            load_plane_quadrant(pl2b, W2_scales, 4, 4, q, True)
 
         w2t = []
         for a in range(4):

@@ -27,15 +27,15 @@ def tile_naivematryoshkalinear_w_kernel(tc, x, W0_words, W0_scales, W1_words, W1
         psum = ctx.enter_context(tc.psum_pool(name="psum", bufs=8))
         ctx.enter_context(tc.manual_schedule())
 
-        xg = xs.tile([P, 8192], BF16, name="xg", tag="xs", align_bytes=64)
+        xg = xs.tile([P, 8192], BF16, name="xg", tag="xs", align_bytes=256)
         x_sb = xg[:, 0:4096]
         grouped = xg[:, 4096:8192].rearrange("p (g m t) -> p g m t", g=8, m=P, t=4)
         nc.sync.dma_start(out=x_sb, in_=xf)
 
-        pl2a = const.tile([P, 4608], U8, name="pl2a", align_bytes=64)
-        pl2b = const.tile([P, 4608], U8, name="pl2b", align_bytes=64)
-        pl1 = const.tile([P, 2048], U8, name="pl1", align_bytes=64)
-        pl0 = const.tile([P, 2048], U8, name="pl0", align_bytes=64)
+        pl2a = const.tile([P, 4608], U8, name="pl2a", align_bytes=256)
+        pl2b = const.tile([P, 4608], U8, name="pl2b", align_bytes=256)
+        pl1 = const.tile([P, 2048], U8, name="pl1", align_bytes=256)
+        pl0 = const.tile([P, 2048], U8, name="pl0", align_bytes=256)
         for pl in (pl2a, pl1, pl0, pl2b):
             nc.vector.memset(pl[:].bitcast(I32), 0)
 
@@ -65,21 +65,21 @@ def tile_naivematryoshkalinear_w_kernel(tc, x, W0_words, W0_scales, W1_words, W1
 
         w2t = []
         for a in range(4):
-            wt = w2pool.tile([P, 2, 4 * 4608], U8, name="w2t", tag="w2", align_bytes=64)
+            wt = w2pool.tile([P, 2, 4 * 4608], U8, name="w2t", tag="w2", align_bytes=256)
             nc.sync.dma_start(out=wt[:].bitcast(I32), in_=W2_words[2 * a : 2 * a + 2].rearrange("g p n t -> p g (n t)").bitcast(I32))
             w2t.append(wt)
         w1t = []
         for a in range(2):
-            wt = wsmall.tile([P, 2, 4 * 2048], U8, name="w1t%d" % a, tag="w1t%d" % a, align_bytes=64)
+            wt = wsmall.tile([P, 2, 4 * 2048], U8, name="w1t%d" % a, tag="w1t%d" % a, align_bytes=256)
             nc.sync.dma_start(out=wt[:].bitcast(I32), in_=W1_words[2 * a : 2 * a + 2].rearrange("g p n t -> p g (n t)").bitcast(I32))
             w1t.append(wt)
-        w0first = wsmall.tile([P, 4 * 2048], U8, name="w0first", tag="w0first", align_bytes=64)
+        w0first = wsmall.tile([P, 4 * 2048], U8, name="w0first", tag="w0first", align_bytes=256)
         nc.sync.dma_start(out=w0first[:].bitcast(I32), in_=W0_words[0].rearrange("p n t -> p (n t)").bitcast(I32))
-        w0last = wsmall.tile([P, 4 * 2048], U8, name="w0last", tag="w0last", align_bytes=64)
+        w0last = wsmall.tile([P, 4 * 2048], U8, name="w0last", tag="w0last", align_bytes=256)
         nc.sync.dma_start(out=w0last[:].bitcast(I32), in_=W0_words[1].rearrange("p n t -> p (n t)").bitcast(I32))
 
-        x_codes = const.tile([P, 8 * P], U32, name="x_codes", align_bytes=64)
-        x_plane = const.tile([P, 8 * P], U8, name="x_plane", align_bytes=64)
+        x_codes = const.tile([P, 8 * P], U32, name="x_codes", align_bytes=256)
+        x_plane = const.tile([P, 8 * P], U8, name="x_plane", align_bytes=256)
         xw = x_sb.bitcast(F32)
         for b in range(4):
             xt = psum.tile([P, 2, 2, P], F32, name="xt", tag="bank")
@@ -129,7 +129,7 @@ def tile_naivematryoshkalinear_w_kernel(tc, x, W0_words, W0_scales, W1_words, W1
             for blk in range(8):
                 c0 = BANK * blk
                 mx_pass(accs[blk][:], g, w2t[g // 2][:, g % 2, 4 * c0 : 4 * (c0 + BANK)], plane2(g, c0), g == 0, g == 7)
-        st_main = xs.tile([P, 4608], F32, name="st_main", tag="xs", align_bytes=64)
+        st_main = xs.tile([P, 4608], F32, name="st_main", tag="xs", align_bytes=256)
         for blk in range(8):
             leave_psum(st_main[:, BANK * blk : BANK * (blk + 1)], accs[blk][:])
 
@@ -137,7 +137,7 @@ def tile_naivematryoshkalinear_w_kernel(tc, x, W0_words, W0_scales, W1_words, W1
         for g in range(8):
             mx_pass(acc8[:], g, w2t[g // 2][:, g % 2, 4 * 4096 : 4 * 4608], plane2(g, 4096), g == 0, g == 7)
         leave_psum(st_main[:, 4096:4608], acc8[:])
-        st_late = w2pool.tile([P, 4096], F32, name="st_late", tag="w2", align_bytes=64)
+        st_late = w2pool.tile([P, 4096], F32, name="st_late", tag="w2", align_bytes=256)
 
         accs = [psum.tile([P, BANK], F32, name="acc", tag="bank") for blk in range(4)]
         for g in range(4):

from contextlib import ExitStack

import concourse.mybir as mybir
from concourse.masks import make_identity

F32 = mybir.dt.float32
BF16 = mybir.dt.bfloat16
I32 = mybir.dt.int32
U8 = mybir.dt.uint8
U32 = mybir.dt.uint32
FP8X4 = mybir.dt.float8_e4m3fn_x4

P = 128
BANK = 512
FLOPS = 2 * 128 * (1024 * 2048 + 2048 * 2048 + 4096 * 4608)


def tile_naivematryoshkalinear_w_kernel(tc, x, W0_words, W0_scales, W1_words, W1_scales, W2_words, W2_scales, out):
    nc = tc.nc
    xf = x.flatten_outer_dims()
    outf = out.flatten_outer_dims()
    with ExitStack() as ctx:
        const = ctx.enter_context(tc.tile_pool(name="const", bufs=1))
        xs = ctx.enter_context(tc.tile_pool(name="xs", bufs=1))
        w2pool = ctx.enter_context(tc.tile_pool(name="w2", bufs=4))
        wsmall = ctx.enter_context(tc.tile_pool(name="ws", bufs=1))
        psum = ctx.enter_context(tc.psum_pool(name="psum", bufs=8))
        ctx.enter_context(tc.manual_schedule())

        xg = xs.tile([P, 8192], BF16, name="xg", tag="xs", align_bytes=256)
        x_sb = xg[:, 0:4096]
        grouped = xg[:, 4096:8192].rearrange("p (g m t) -> p g m t", g=8, m=P, t=4)
        nc.sync.dma_start(out=x_sb, in_=xf)

        pl2a = const.tile([P, 4608], U8, name="pl2a", align_bytes=256)
        pl2b = const.tile([P, 4608], U8, name="pl2b", align_bytes=256)
        pl1 = const.tile([P, 2048], U8, name="pl1", align_bytes=256)
        pl0 = const.tile([P, 2048], U8, name="pl0", align_bytes=256)
        for pl in (pl2a, pl1, pl0, pl2b):
            nc.vector.memset(pl[:].bitcast(I32), 0)

        ident = const.tile([P, P], F32, name="ident")
        make_identity(nc, ident[:])

        def load_plane_quadrant(pl, scales, g0, count, q, software):
            dst = pl[32 * q : 32 * q + 4 * count, :]
            src = scales[g0 : g0 + count, 4 * q : 4 * q + 4, :]
            if software:
                nc.gpsimd.dma_start(out=dst.bitcast(F32), in_=src.bitcast(F32))
            else:
                nc.sync.dma_start(out=dst.bitcast(I32), in_=src.bitcast(I32))

        first_half = [(pl2a, W2_scales, 0, 4), (pl1, W1_scales, 0, 4), (pl0, W0_scales, 0, 2)]
        second_half = [(pl2b, W2_scales, 4, 4), (pl1, W1_scales, 0, 4), (pl0, W0_scales, 0, 2)]
        for pl, scales, g0, count in first_half:
            for q in (2, 3):
                load_plane_quadrant(pl, scales, g0, count, q, False)
        for q in (0, 1):
            load_plane_quadrant(pl2a, W2_scales, 0, 4, q, True)
        for pl, scales, g0, count in second_half:
            for q in (0, 1):
                load_plane_quadrant(pl, scales, g0, count, q, False)
        for q in (2, 3):
            load_plane_quadrant(pl2b, W2_scales, 4, 4, q, True)

        w2t = []
        for a in range(4):
            wt = w2pool.tile([P, 2, 4 * 4608], U8, name="w2t", tag="w2", align_bytes=256)
            nc.sync.dma_start(out=wt[:].bitcast(I32), in_=W2_words[2 * a : 2 * a + 2].rearrange("g p n t -> p g (n t)").bitcast(I32))
            w2t.append(wt)
        w1t = []
        for a in range(2):
            wt = wsmall.tile([P, 2, 4 * 2048], U8, name="w1t%d" % a, tag="w1t%d" % a, align_bytes=256)
            nc.sync.dma_start(out=wt[:].bitcast(I32), in_=W1_words[2 * a : 2 * a + 2].rearrange("g p n t -> p g (n t)").bitcast(I32))
            w1t.append(wt)
        w0first = wsmall.tile([P, 4 * 2048], U8, name="w0first", tag="w0first", align_bytes=256)
        nc.sync.dma_start(out=w0first[:].bitcast(I32), in_=W0_words[0].rearrange("p n t -> p (n t)").bitcast(I32))
        w0last = wsmall.tile([P, 4 * 2048], U8, name="w0last", tag="w0last", align_bytes=256)
        nc.sync.dma_start(out=w0last[:].bitcast(I32), in_=W0_words[1].rearrange("p n t -> p (n t)").bitcast(I32))

        x_codes = const.tile([P, 8 * P], U32, name="x_codes", align_bytes=256)
        x_plane = const.tile([P, 8 * P], U8, name="x_plane", align_bytes=256)
        xw = x_sb.bitcast(F32)
        for b in range(4):
            xt = psum.tile([P, 2, 2, P], F32, name="xt", tag="bank")
            for gg in range(2):
                g = 2 * b + gg
                for u in range(2):
                    nc.tensor.transpose(xt[:, gg, u, :], xw[:, 256 * g + u : 256 * (g + 1) : 2], ident[:])
            dst = grouped[:, 2 * b : 2 * b + 2].bitcast(F32)
            src = xt[:].rearrange("p g u m -> p g m u")
            if b % 2 == 0:
                nc.vector.tensor_copy(out=dst, in_=src)
            else:
                nc.scalar.copy(out=dst, in_=src)
        for b in range(4):
            nc.vector.quantize_mx(
                out=x_codes[:, 256 * b : 256 * (b + 1)].bitcast(FP8X4),
                scales=x_plane[:, 256 * b : 256 * (b + 1)],
                in_=xg[:, 4096 + 1024 * b : 4096 + 1024 * (b + 1)],
            )

        state = {"copies": 0}

        def mx_pass(acc, g, codes, plane, first, last):
            nc.tensor.matmul_mx(
                out=acc,
                lhsT=x_codes[:, P * g : P * (g + 1)].bitcast(FP8X4),
                lhsT_scale=x_plane[:, P * g : P * (g + 1)],
                rhs=codes.bitcast(FP8X4),
                rhs_scale=plane,
                start=first,
                stop=last,
            )

        def leave_psum(dst, acc):
            if state["copies"] % 2 == 0:
                nc.vector.tensor_copy(out=dst, in_=acc)
            else:
                nc.scalar.copy(out=dst, in_=acc)
            state["copies"] += 1

        def plane2(g, c0):
            pl = pl2a if g < 4 else pl2b
            return pl[4 * (g % 4) : P, c0 : c0 + BANK]

        accs = [psum.tile([P, BANK], F32, name="acc", tag="bank") for blk in range(8)]
        for g in range(8):
            for blk in range(8):
                c0 = BANK * blk
                mx_pass(accs[blk][:], g, w2t[g // 2][:, g % 2, 4 * c0 : 4 * (c0 + BANK)], plane2(g, c0), g == 0, g == 7)
        st_main = xs.tile([P, 4608], F32, name="st_main", tag="xs", align_bytes=256)
        for blk in range(8):
            leave_psum(st_main[:, BANK * blk : BANK * (blk + 1)], accs[blk][:])

        acc8 = psum.tile([P, BANK], F32, name="acc", tag="bank")
        for g in range(8):
            mx_pass(acc8[:], g, w2t[g // 2][:, g % 2, 4 * 4096 : 4 * 4608], plane2(g, 4096), g == 0, g == 7)
        leave_psum(st_main[:, 4096:4608], acc8[:])
        st_late = w2pool.tile([P, 4096], F32, name="st_late", tag="w2", align_bytes=256)

        accs = [psum.tile([P, BANK], F32, name="acc", tag="bank") for blk in range(4)]
        for g in range(4):
            for blk in range(4):
                c0 = BANK * blk
                mx_pass(accs[blk][:], g, w1t[g // 2][:, g % 2, 4 * c0 : 4 * (c0 + BANK)], pl1[4 * g : P, c0 : c0 + BANK], g == 0, g == 3)
        for blk in range(4):
            leave_psum(st_late[:, 2048 + BANK * blk : 2048 + BANK * (blk + 1)], accs[blk][:])

        accs = [psum.tile([P, BANK], F32, name="acc", tag="bank") for blk in range(4)]
        for blk in range(4):
            c0 = BANK * blk
            mx_pass(accs[blk][:], 0, w0first[:, 4 * c0 : 4 * (c0 + BANK)], pl0[0:P, c0 : c0 + BANK], True, False)
        for blk in range(4):
            c0 = BANK * blk
            mx_pass(accs[blk][:], 1, w0last[:, 4 * c0 : 4 * (c0 + BANK)], pl0[4:P, c0 : c0 + BANK], False, True)
            leave_psum(st_late[:, c0 : c0 + BANK], accs[blk][:])

        nc.sync.dma_start(out=outf[:, 4096:8704], in_=st_main[:])
        nc.sync.dma_start(out=outf[:, 2048:4096], in_=st_late[:, 2048:4096])
        nc.sync.dma_start(out=outf[:, 0:2048], in_=st_late[:, 0:2048])
